import numpy as np
import ml_dtypes

BF16 = ml_dtypes.bfloat16


def bf(x):
    return np.asarray(x, np.float32).astype(BF16)


def f32(x):
    return np.asarray(x, np.float32)


def f64(x):
    return np.asarray(x).astype(np.float64)


def striped(idx):
    return np.tile(idx.reshape(-1, 16).T, (8, 1))


C, S, N = 256, 4096, 512


def setup_inputs():
    emb = f32(0.25 * np.random.standard_normal((C, S)) * (0.5 + np.random.random((1, S))))
    w = bf(0.25 * np.random.standard_normal((C, C)))
    return {"emb": emb, "w": w, "offs": striped(np.random.permutation(S)[:N])}


def reference(emb, w, offs):
    idx = offs[:16].T.reshape(-1)
    r = f64(emb)[:, idx]
    x = r / np.sqrt(np.sum(r * r, axis=0, keepdims=True))
    f = np.maximum(f64(w).T @ x, 0.0)
    return np.concatenate([x, f], axis=0)

@@ -1,0 +1,66 @@
+import concourse.mybir as mybir
+
+P = 128
+C, S, N = 256, 4096, 512
+BLOCKS = C // P
+F32, BF16, U16 = mybir.dt.float32, mybir.dt.bfloat16, mybir.dt.uint16
+ACT = mybir.ActivationFunctionType
+MULT = mybir.AluOpType.mult
+
+FLOPS = 2 * C * C * N
+
+
+def tile_decomposeable_kernel(tc, emb, w, offs, out):
+    nc = tc.nc
+    with (
+        tc.tile_pool(name="held", bufs=1) as held,
+        tc.psum_pool(name="psum", bufs=1) as psum,
+    ):
+        offsets = held.tile([P, N // 16], U16, name="offsets")
+        nc.sync.dma_start(offsets[:], offs)
+        table = [held.tile([P, S], F32, name=f"table{b}") for b in range(BLOCKS)]
+        for b in range(BLOCKS):
+            nc.sync.dma_start(table[b][:], emb[b * P : (b + 1) * P, :])
+        weights = [held.tile([P, C], BF16, name=f"weights{b}") for b in range(BLOCKS)]
+        for b in range(BLOCKS):
+            nc.sync.dma_start(weights[b][:], w[b * P : (b + 1) * P, :])
+
+        ones = held.tile([P, P], F32, name="ones")
+        nc.vector.memset(ones[:], 1.0)
+        warm = held.tile([P, 1], F32, name="warm")
+        nc.scalar.activation(warm[:], ones[:, 0:1], ACT.Abs_reciprocal_sqrt)
+
+        picked = [held.tile([P, N], F32, name=f"picked{b}") for b in range(BLOCKS)]
+        squares = [held.tile([P, N], F32, name=f"squares{b}") for b in range(BLOCKS)]
+        sumsq = psum.tile([P, N], F32, name="sumsq")
+        for b in range(BLOCKS):
+            nc.scalar.activation(picked[b][:], table[b][:].indirect(offsets[:]), ACT.Copy)
+            nc.vector.tensor_tensor(squares[b][:], picked[b][:], picked[b][:], MULT)
+            nc.tensor.matmul(sumsq[:], ones[:], squares[b][:], start=(b == 0), stop=(b == BLOCKS - 1))
+
+        inverse = held.tile([P, N], F32, name="inverse")
+        nc.scalar.activation(inverse[:], sumsq[:], ACT.Abs_reciprocal_sqrt)
+
+        unit_bf = [held.tile([P, N], BF16, name=f"unit_bf{b}") for b in range(BLOCKS)]
+        for b in range(BLOCKS):
+            nc.vector.tensor_tensor(unit_bf[b][:], picked[b][:], inverse[:], MULT)
+        unit = [held.tile([P, N], F32, name=f"unit{b}") for b in range(BLOCKS)]
+        for b in range(BLOCKS):
+            nc.vector.tensor_tensor(unit[b][:], picked[b][:], inverse[:], MULT)
+            nc.sync.dma_start(out[b * P : (b + 1) * P, :], unit[b][:])
+
+        product = [psum.tile([P, N], F32, name=f"product{m}") for m in range(BLOCKS)]
+        for b in range(BLOCKS):
+            for m in range(BLOCKS):
+                nc.tensor.matmul(
+                    product[m][:],
+                    weights[b][:, m * P : (m + 1) * P],
+                    unit_bf[b][:],
+                    start=(b == 0),
+                    stop=(b == BLOCKS - 1),
+                )
+        features = [held.tile([P, N], F32, name=f"features{m}") for m in range(BLOCKS)]
+        nc.scalar.activation(features[0][:], product[0][:], ACT.Relu)
+        nc.vector.tensor_scalar_max(features[1][:], product[1][:], 0.0)
+        nc.sync.dma_start(out[C : C + P, :], features[0][:])
+        nc.scalar.dma_start(out[C + P : C + 2 * P, :], features[1][:])

@@ -33,7 +33,9 @@ def tile_decomposeable_kernel(tc, emb, w, offs, out):
         picked = [held.tile([P, N], F32, name=f"picked{b}") for b in range(BLOCKS)]
         squares = [held.tile([P, N], F32, name=f"squares{b}") for b in range(BLOCKS)]
         sumsq = psum.tile([P, N], F32, name="sumsq")
+        unread = psum.tile([P, N], F32, name="unread")
         for b in range(BLOCKS):
+            nc.tensor.matmul(unread[:], ones[:], table[b][:, 0:N], start=True, stop=True)
             nc.scalar.activation(picked[b][:], table[b][:].indirect(offsets[:]), ACT.Copy)
             nc.vector.tensor_tensor(squares[b][:], picked[b][:], picked[b][:], MULT)
             nc.tensor.matmul(sumsq[:], ones[:], squares[b][:], start=(b == 0), stop=(b == BLOCKS - 1))

@@ -3,6 +3,8 @@ import concourse.mybir as mybir
 P = 128
 C, S, N = 256, 4096, 512
 BLOCKS = C // P
+PIECES = 2
+W = N // PIECES
 F32, BF16, U16 = mybir.dt.float32, mybir.dt.bfloat16, mybir.dt.uint16
 ACT = mybir.ActivationFunctionType
 MULT = mybir.AluOpType.mult
@@ -30,39 +32,44 @@ def tile_decomposeable_kernel(tc, emb, w, offs, out):
         warm = held.tile([P, 1], F32, name="warm")
         nc.scalar.activation(warm[:], ones[:, 0:1], ACT.Abs_reciprocal_sqrt)
 
+        cols = [slice(i * W, (i + 1) * W) for i in range(PIECES)]
+
         picked = [held.tile([P, N], F32, name=f"picked{b}") for b in range(BLOCKS)]
         squares = [held.tile([P, N], F32, name=f"squares{b}") for b in range(BLOCKS)]
-        sumsq = psum.tile([P, N], F32, name="sumsq")
+        sumsq = [psum.tile([P, W], F32, name=f"sumsq{i}") for i in range(PIECES)]
         unread = psum.tile([P, N], F32, name="unread")
         for b in range(BLOCKS):
             nc.tensor.matmul(unread[:], ones[:], table[b][:, 0:N], start=True, stop=True)
             nc.scalar.activation(picked[b][:], table[b][:].indirect(offsets[:]), ACT.Copy)
-            nc.vector.tensor_tensor(squares[b][:], picked[b][:], picked[b][:], MULT)
-            nc.tensor.matmul(sumsq[:], ones[:], squares[b][:], start=(b == 0), stop=(b == BLOCKS - 1))
+            for i in range(PIECES):
+                nc.vector.tensor_tensor(squares[b][:, cols[i]], picked[b][:, cols[i]], picked[b][:, cols[i]], MULT)
+                nc.tensor.matmul(
+                    sumsq[i][:], ones[:], squares[b][:, cols[i]], start=(b == 0), stop=(b == BLOCKS - 1)
+                )
 
         inverse = held.tile([P, N], F32, name="inverse")
-        nc.scalar.activation(inverse[:], sumsq[:], ACT.Abs_reciprocal_sqrt)
-
         unit_bf = [held.tile([P, N], BF16, name=f"unit_bf{b}") for b in range(BLOCKS)]
-        for b in range(BLOCKS):
-            nc.vector.tensor_tensor(unit_bf[b][:], picked[b][:], inverse[:], MULT)
+        product = [[psum.tile([P, W], F32, name=f"product{m}_{i}") for i in range(PIECES)] for m in range(BLOCKS)]
+        for i in range(PIECES):
+            nc.scalar.activation(inverse[:, cols[i]], sumsq[i][:], ACT.Abs_reciprocal_sqrt)
+            for b in range(BLOCKS):
+                nc.vector.tensor_tensor(unit_bf[b][:, cols[i]], picked[b][:, cols[i]], inverse[:, cols[i]], MULT)
+                for m in range(BLOCKS):
+                    nc.tensor.matmul(
+                        product[m][i][:],
+                        weights[b][:, m * P : (m + 1) * P],
+                        unit_bf[b][:, cols[i]],
+                        start=(b == 0),
+                        stop=(b == BLOCKS - 1),
+                    )
+
         unit = [held.tile([P, N], F32, name=f"unit{b}") for b in range(BLOCKS)]
         for b in range(BLOCKS):
             nc.vector.tensor_tensor(unit[b][:], picked[b][:], inverse[:], MULT)
             nc.sync.dma_start(out[b * P : (b + 1) * P, :], unit[b][:])
 
-        product = [psum.tile([P, N], F32, name=f"product{m}") for m in range(BLOCKS)]
-        for b in range(BLOCKS):
-            for m in range(BLOCKS):
-                nc.tensor.matmul(
-                    product[m][:],
-                    weights[b][:, m * P : (m + 1) * P],
-                    unit_bf[b][:],
-                    start=(b == 0),
-                    stop=(b == BLOCKS - 1),
-                )
         features = [held.tile([P, N], F32, name=f"features{m}") for m in range(BLOCKS)]
-        nc.scalar.activation(features[0][:], product[0][:], ACT.Relu)
-        nc.vector.tensor_scalar_max(features[1][:], product[1][:], 0.0)
-        nc.sync.dma_start(out[C : C + P, :], features[0][:])
-        nc.scalar.dma_start(out[C + P : C + 2 * P, :], features[1][:])
+        for i in range(PIECES):
+            for m in range(BLOCKS):
+                nc.scalar.activation(features[m][:, cols[i]], product[m][i][:], ACT.Relu)
+                nc.sync.dma_start(out[C + m * P : C + (m + 1) * P, cols[i]], features[m][:, cols[i]])

@@ -48,12 +48,20 @@ def tile_decomposeable_kernel(tc, emb, w, offs, out):
                 )
 
         inverse = held.tile([P, N], F32, name="inverse")
+        for i in range(PIECES):
+            nc.scalar.activation(inverse[:, cols[i]], sumsq[i][:], ACT.Abs_reciprocal_sqrt)
+
+        unit = [held.tile([P, N], F32, name=f"unit{b}") for b in range(BLOCKS)]
         unit_bf = [held.tile([P, N], BF16, name=f"unit_bf{b}") for b in range(BLOCKS)]
         product = [[psum.tile([P, W], F32, name=f"product{m}_{i}") for i in range(PIECES)] for m in range(BLOCKS)]
         for i in range(PIECES):
-            nc.scalar.activation(inverse[:, cols[i]], sumsq[i][:], ACT.Abs_reciprocal_sqrt)
             for b in range(BLOCKS):
-                nc.vector.tensor_tensor(unit_bf[b][:, cols[i]], picked[b][:, cols[i]], inverse[:, cols[i]], MULT)
+                nc.vector.tensor_tensor(unit[b][:, cols[i]], picked[b][:, cols[i]], inverse[:, cols[i]], MULT)
+                nc.sync.dma_start(out[b * P : (b + 1) * P, cols[i]], unit[b][:, cols[i]])
+                if b == 0:
+                    nc.scalar.activation(unit_bf[b][:, cols[i]], unit[b][:, cols[i]], ACT.Copy)
+                else:
+                    nc.vector.tensor_copy(unit_bf[b][:, cols[i]], unit[b][:, cols[i]])
                 for m in range(BLOCKS):
                     nc.tensor.matmul(
                         product[m][i][:],
@@ -63,13 +71,9 @@ def tile_decomposeable_kernel(tc, emb, w, offs, out):
                         stop=(b == BLOCKS - 1),
                     )
 
-        unit = [held.tile([P, N], F32, name=f"unit{b}") for b in range(BLOCKS)]
-        for b in range(BLOCKS):
-            nc.vector.tensor_tensor(unit[b][:], picked[b][:], inverse[:], MULT)
-            nc.sync.dma_start(out[b * P : (b + 1) * P, :], unit[b][:])
-
         features = [held.tile([P, N], F32, name=f"features{m}") for m in range(BLOCKS)]
         for i in range(PIECES):
+            nc.scalar.activation(features[0][:, cols[i]], product[0][i][:], ACT.Relu)
+            nc.vector.tensor_scalar_max(features[1][:, cols[i]], product[1][i][:], 0.0)
             for m in range(BLOCKS):
-                nc.scalar.activation(features[m][:, cols[i]], product[m][i][:], ACT.Relu)
                 nc.sync.dma_start(out[C + m * P : C + (m + 1) * P, cols[i]], features[m][:, cols[i]])

@@ -3,7 +3,7 @@ import concourse.mybir as mybir
 P = 128
 C, S, N = 256, 4096, 512
 BLOCKS = C // P
-PIECES = 2
+PIECES = 4
 W = N // PIECES
 F32, BF16, U16 = mybir.dt.float32, mybir.dt.bfloat16, mybir.dt.uint16
 ACT = mybir.ActivationFunctionType
@@ -17,6 +17,7 @@ def tile_decomposeable_kernel(tc, emb, w, offs, out):
     with (
         tc.tile_pool(name="held", bufs=1) as held,
         tc.psum_pool(name="psum", bufs=1) as psum,
+        tc.psum_pool(name="turns", bufs=2) as turns,
     ):
         offsets = held.tile([P, N // 16], U16, name="offsets")
         nc.sync.dma_start(offsets[:], offs)
@@ -33,12 +34,13 @@ def tile_decomposeable_kernel(tc, emb, w, offs, out):
         nc.scalar.activation(warm[:], ones[:, 0:1], ACT.Abs_reciprocal_sqrt)
 
         cols = [slice(i * W, (i + 1) * W) for i in range(PIECES)]
+        pair = [slice(g * 2 * W, (g + 1) * 2 * W) for g in range(PIECES // 2)]
 
         picked = [held.tile([P, N], F32, name=f"picked{b}") for b in range(BLOCKS)]
         squares = [held.tile([P, N], F32, name=f"squares{b}") for b in range(BLOCKS)]
         sumsq = [psum.tile([P, W], F32, name=f"sumsq{i}") for i in range(PIECES)]
-        unread = psum.tile([P, N], F32, name="unread")
         for b in range(BLOCKS):
+            unread = turns.tile([P, N], F32, name="unread", tag="product0")
             nc.tensor.matmul(unread[:], ones[:], table[b][:, 0:N], start=True, stop=True)
             nc.scalar.activation(picked[b][:], table[b][:].indirect(offsets[:]), ACT.Copy)
             for i in range(PIECES):
@@ -53,27 +55,31 @@ def tile_decomposeable_kernel(tc, emb, w, offs, out):
 
         unit = [held.tile([P, N], F32, name=f"unit{b}") for b in range(BLOCKS)]
         unit_bf = [held.tile([P, N], BF16, name=f"unit_bf{b}") for b in range(BLOCKS)]
-        product = [[psum.tile([P, W], F32, name=f"product{m}_{i}") for i in range(PIECES)] for m in range(BLOCKS)]
-        for i in range(PIECES):
-            for b in range(BLOCKS):
-                nc.vector.tensor_tensor(unit[b][:, cols[i]], picked[b][:, cols[i]], inverse[:, cols[i]], MULT)
-                nc.sync.dma_start(out[b * P : (b + 1) * P, cols[i]], unit[b][:, cols[i]])
-                if b == 0:
-                    nc.scalar.activation(unit_bf[b][:, cols[i]], unit[b][:, cols[i]], ACT.Copy)
-                else:
-                    nc.vector.tensor_copy(unit_bf[b][:, cols[i]], unit[b][:, cols[i]])
-                for m in range(BLOCKS):
-                    nc.tensor.matmul(
-                        product[m][i][:],
-                        weights[b][:, m * P : (m + 1) * P],
-                        unit_bf[b][:, cols[i]],
-                        start=(b == 0),
-                        stop=(b == BLOCKS - 1),
-                    )
-
         features = [held.tile([P, N], F32, name=f"features{m}") for m in range(BLOCKS)]
-        for i in range(PIECES):
-            nc.scalar.activation(features[0][:, cols[i]], product[0][i][:], ACT.Relu)
-            nc.vector.tensor_scalar_max(features[1][:, cols[i]], product[1][i][:], 0.0)
-            for m in range(BLOCKS):
-                nc.sync.dma_start(out[C + m * P : C + (m + 1) * P, cols[i]], features[m][:, cols[i]])
+        product = []
+        for i in range(PIECES + 1):
+            if i < PIECES:
+                product.append([turns.tile([P, N], F32, name=f"product{m}", tag=f"product{m}") for m in range(BLOCKS)])
+                for b in range(BLOCKS):
+                    nc.vector.tensor_tensor(unit[b][:, cols[i]], picked[b][:, cols[i]], inverse[:, cols[i]], MULT)
+                    if i % 2 == 1:
+                        nc.sync.dma_start(out[b * P : (b + 1) * P, pair[i // 2]], unit[b][:, pair[i // 2]])
+                    if b == 0:
+                        nc.scalar.activation(unit_bf[b][:, cols[i]], unit[b][:, cols[i]], ACT.Copy)
+                    else:
+                        nc.vector.tensor_copy(unit_bf[b][:, cols[i]], unit[b][:, cols[i]])
+                    for m in range(BLOCKS):
+                        nc.tensor.matmul(
+                            product[i][m][:, 0:W],
+                            weights[b][:, m * P : (m + 1) * P],
+                            unit_bf[b][:, cols[i]],
+                            start=(b == 0),
+                            stop=(b == BLOCKS - 1),
+                        )
+            if i > 0:
+                j = i - 1
+                nc.scalar.activation(features[0][:, cols[j]], product[j][0][:, 0:W], ACT.Relu)
+                nc.vector.tensor_scalar_max(features[1][:, cols[j]], product[j][1][:, 0:W], 0.0)
+                if j % 2 == 1:
+                    for m in range(BLOCKS):
+                        nc.sync.dma_start(out[C + m * P : C + (m + 1) * P, pair[j // 2]], features[m][:, pair[j // 2]])

@@ -42,8 +42,12 @@ def tile_decomposeable_kernel(tc, emb, w, offs, out):
         for b in range(BLOCKS):
             unread = turns.tile([P, N], F32, name="unread", tag="product0")
             nc.tensor.matmul(unread[:], ones[:], table[b][:, 0:N], start=True, stop=True)
-            nc.scalar.activation(picked[b][:], table[b][:].indirect(offsets[:]), ACT.Copy)
             for i in range(PIECES):
+                nc.scalar.activation(
+                    picked[b][:, cols[i]],
+                    table[b][:].indirect(offsets[:, i * (W // 16) : (i + 1) * (W // 16)]),
+                    ACT.Copy,
+                )
                 nc.vector.tensor_tensor(squares[b][:, cols[i]], picked[b][:, cols[i]], picked[b][:, cols[i]], MULT)
                 nc.tensor.matmul(
                     sumsq[i][:], ones[:], squares[b][:, cols[i]], start=(b == 0), stop=(b == BLOCKS - 1)

@@ -20,10 +20,10 @@ def tile_decomposeable_kernel(tc, emb, w, offs, out):
         tc.psum_pool(name="turns", bufs=2) as turns,
     ):
         offsets = held.tile([P, N // 16], U16, name="offsets")
-        nc.sync.dma_start(offsets[:], offs)
         table = [held.tile([P, S], F32, name=f"table{b}") for b in range(BLOCKS)]
-        for b in range(BLOCKS):
-            nc.sync.dma_start(table[b][:], emb[b * P : (b + 1) * P, :])
+        nc.sync.dma_start(table[0][:], emb[0:P, :])
+        nc.sync.dma_start(offsets[:], offs)
+        nc.sync.dma_start(table[1][:], emb[P : 2 * P, :])
         weights = [held.tile([P, C], BF16, name=f"weights{b}") for b in range(BLOCKS)]
         for b in range(BLOCKS):
             nc.sync.dma_start(weights[b][:], w[b * P : (b + 1) * P, :])
@@ -65,13 +65,7 @@ def tile_decomposeable_kernel(tc, emb, w, offs, out):
             if i < PIECES:
                 product.append([turns.tile([P, N], F32, name=f"product{m}", tag=f"product{m}") for m in range(BLOCKS)])
                 for b in range(BLOCKS):
-                    nc.vector.tensor_tensor(unit[b][:, cols[i]], picked[b][:, cols[i]], inverse[:, cols[i]], MULT)
-                    if i % 2 == 1:
-                        nc.sync.dma_start(out[b * P : (b + 1) * P, pair[i // 2]], unit[b][:, pair[i // 2]])
-                    if b == 0:
-                        nc.scalar.activation(unit_bf[b][:, cols[i]], unit[b][:, cols[i]], ACT.Copy)
-                    else:
-                        nc.vector.tensor_copy(unit_bf[b][:, cols[i]], unit[b][:, cols[i]])
+                    nc.vector.tensor_tensor(unit_bf[b][:, cols[i]], picked[b][:, cols[i]], inverse[:, cols[i]], MULT)
                     for m in range(BLOCKS):
                         nc.tensor.matmul(
                             product[i][m][:, 0:W],
@@ -82,8 +76,11 @@ def tile_decomposeable_kernel(tc, emb, w, offs, out):
                         )
             if i > 0:
                 j = i - 1
-                nc.scalar.activation(features[0][:, cols[j]], product[j][0][:, 0:W], ACT.Relu)
-                nc.vector.tensor_scalar_max(features[1][:, cols[j]], product[j][1][:, 0:W], 0.0)
-                if j % 2 == 1:
-                    for m in range(BLOCKS):
+                for b in range(BLOCKS):
+                    nc.vector.tensor_tensor(unit[b][:, cols[j]], picked[b][:, cols[j]], inverse[:, cols[j]], MULT)
+                    if j % 2 == 1:
+                        nc.sync.dma_start(out[b * P : (b + 1) * P, pair[j // 2]], unit[b][:, pair[j // 2]])
+                for m in range(BLOCKS):
+                    nc.scalar.activation(features[m][:, cols[j]], product[j][m][:, 0:W], ACT.Relu)
+                    if j % 2 == 1:
                         nc.sync.dma_start(out[C + m * P : C + (m + 1) * P, pair[j // 2]], features[m][:, pair[j // 2]])

@@ -60,10 +60,11 @@ def tile_decomposeable_kernel(tc, emb, w, offs, out):
         unit = [held.tile([P, N], F32, name=f"unit{b}") for b in range(BLOCKS)]
         unit_bf = [held.tile([P, N], BF16, name=f"unit_bf{b}") for b in range(BLOCKS)]
         features = [held.tile([P, N], F32, name=f"features{m}") for m in range(BLOCKS)]
-        product = []
-        for i in range(PIECES + 1):
-            if i < PIECES:
-                product.append([turns.tile([P, N], F32, name=f"product{m}", tag=f"product{m}") for m in range(BLOCKS)])
+        for g in range(PIECES // 2):
+            members = [2 * g, 2 * g + 1]
+            product = {}
+            for i in members:
+                product[i] = [turns.tile([P, N], F32, name=f"product{m}", tag=f"product{m}") for m in range(BLOCKS)]
                 for b in range(BLOCKS):
                     nc.vector.tensor_tensor(unit_bf[b][:, cols[i]], picked[b][:, cols[i]], inverse[:, cols[i]], MULT)
                     for m in range(BLOCKS):
@@ -74,13 +75,12 @@ def tile_decomposeable_kernel(tc, emb, w, offs, out):
                             start=(b == 0),
                             stop=(b == BLOCKS - 1),
                         )
-            if i > 0:
-                j = i - 1
-                for b in range(BLOCKS):
-                    nc.vector.tensor_tensor(unit[b][:, cols[j]], picked[b][:, cols[j]], inverse[:, cols[j]], MULT)
-                    if j % 2 == 1:
-                        nc.sync.dma_start(out[b * P : (b + 1) * P, pair[j // 2]], unit[b][:, pair[j // 2]])
+            for b in range(BLOCKS):
+                for i in members:
+                    nc.vector.tensor_tensor(unit[b][:, cols[i]], picked[b][:, cols[i]], inverse[:, cols[i]], MULT)
+                nc.sync.dma_start(out[b * P : (b + 1) * P, pair[g]], unit[b][:, pair[g]])
+            for i in members:
                 for m in range(BLOCKS):
-                    nc.scalar.activation(features[m][:, cols[j]], product[j][m][:, 0:W], ACT.Relu)
-                    if j % 2 == 1:
-                        nc.sync.dma_start(out[C + m * P : C + (m + 1) * P, pair[j // 2]], features[m][:, pair[j // 2]])
+                    nc.scalar.activation(features[m][:, cols[i]], product[i][m][:, 0:W], ACT.Relu)
+            for m in range(BLOCKS):
+                nc.sync.dma_start(out[C + m * P : C + (m + 1) * P, pair[g]], features[m][:, pair[g]])

@@ -36,7 +36,7 @@ def tile_decomposeable_kernel(tc, emb, w, offs, out):
         cols = [slice(i * W, (i + 1) * W) for i in range(PIECES)]
         pair = [slice(g * 2 * W, (g + 1) * 2 * W) for g in range(PIECES // 2)]
 
-        picked = [held.tile([P, N], F32, name=f"picked{b}") for b in range(BLOCKS)]
+        picked = held.tile([P, BLOCKS, N], F32, name="picked")
         squares = [held.tile([P, N], F32, name=f"squares{b}") for b in range(BLOCKS)]
         sumsq = [psum.tile([P, W], F32, name=f"sumsq{i}") for i in range(PIECES)]
         for b in range(BLOCKS):
@@ -44,11 +44,11 @@ def tile_decomposeable_kernel(tc, emb, w, offs, out):
             nc.tensor.matmul(unread[:], ones[:], table[b][:, 0:N], start=True, stop=True)
             for i in range(PIECES):
                 nc.scalar.activation(
-                    picked[b][:, cols[i]],
+                    picked[:, b, cols[i]],
                     table[b][:].indirect(offsets[:, i * (W // 16) : (i + 1) * (W // 16)]),
                     ACT.Copy,
                 )
-                nc.vector.tensor_tensor(squares[b][:, cols[i]], picked[b][:, cols[i]], picked[b][:, cols[i]], MULT)
+                nc.vector.tensor_tensor(squares[b][:, cols[i]], picked[:, b, cols[i]], picked[:, b, cols[i]], MULT)
                 nc.tensor.matmul(
                     sumsq[i][:], ones[:], squares[b][:, cols[i]], start=(b == 0), stop=(b == BLOCKS - 1)
                 )
@@ -58,26 +58,26 @@ def tile_decomposeable_kernel(tc, emb, w, offs, out):
             nc.scalar.activation(inverse[:, cols[i]], sumsq[i][:], ACT.Abs_reciprocal_sqrt)
 
         unit = [held.tile([P, N], F32, name=f"unit{b}") for b in range(BLOCKS)]
-        unit_bf = [held.tile([P, N], BF16, name=f"unit_bf{b}") for b in range(BLOCKS)]
+        unit_bf = held.tile([P, BLOCKS, N], BF16, name="unit_bf")
         features = [held.tile([P, N], F32, name=f"features{m}") for m in range(BLOCKS)]
         for g in range(PIECES // 2):
             members = [2 * g, 2 * g + 1]
             product = {}
             for i in members:
                 product[i] = [turns.tile([P, N], F32, name=f"product{m}", tag=f"product{m}") for m in range(BLOCKS)]
-                for b in range(BLOCKS):
-                    nc.vector.tensor_tensor(unit_bf[b][:, cols[i]], picked[b][:, cols[i]], inverse[:, cols[i]], MULT)
-                    for m in range(BLOCKS):
+                both = inverse[:, cols[i]].unsqueeze(1).to_broadcast([P, BLOCKS, W])
+                nc.vector.tensor_tensor(unit_bf[:, :, cols[i]], picked[:, :, cols[i]], both, MULT)
+                for m in range(BLOCKS):
+                    for b in range(BLOCKS):
                         nc.tensor.matmul(
                             product[i][m][:, 0:W],
                             weights[b][:, m * P : (m + 1) * P],
-                            unit_bf[b][:, cols[i]],
+                            unit_bf[:, b, cols[i]],
                             start=(b == 0),
                             stop=(b == BLOCKS - 1),
                         )
             for b in range(BLOCKS):
-                for i in members:
-                    nc.vector.tensor_tensor(unit[b][:, cols[i]], picked[b][:, cols[i]], inverse[:, cols[i]], MULT)
+                nc.vector.tensor_tensor(unit[b][:, pair[g]], picked[:, b, pair[g]], inverse[:, pair[g]], MULT)
                 nc.sync.dma_start(out[b * P : (b + 1) * P, pair[g]], unit[b][:, pair[g]])
             for i in members:
                 for m in range(BLOCKS):

@@ -34,7 +34,6 @@ def tile_decomposeable_kernel(tc, emb, w, offs, out):
         nc.scalar.activation(warm[:], ones[:, 0:1], ACT.Abs_reciprocal_sqrt)
 
         cols = [slice(i * W, (i + 1) * W) for i in range(PIECES)]
-        pair = [slice(g * 2 * W, (g + 1) * 2 * W) for g in range(PIECES // 2)]
 
         picked = held.tile([P, BLOCKS, N], F32, name="picked")
         squares = [held.tile([P, N], F32, name=f"squares{b}") for b in range(BLOCKS)]
@@ -60,27 +59,27 @@ def tile_decomposeable_kernel(tc, emb, w, offs, out):
         unit = [held.tile([P, N], F32, name=f"unit{b}") for b in range(BLOCKS)]
         unit_bf = held.tile([P, BLOCKS, N], BF16, name="unit_bf")
         features = [held.tile([P, N], F32, name=f"features{m}") for m in range(BLOCKS)]
-        for g in range(PIECES // 2):
-            members = [2 * g, 2 * g + 1]
-            product = {}
-            for i in members:
-                product[i] = [turns.tile([P, N], F32, name=f"product{m}", tag=f"product{m}") for m in range(BLOCKS)]
-                both = inverse[:, cols[i]].unsqueeze(1).to_broadcast([P, BLOCKS, W])
-                nc.vector.tensor_tensor(unit_bf[:, :, cols[i]], picked[:, :, cols[i]], both, MULT)
-                for m in range(BLOCKS):
-                    for b in range(BLOCKS):
-                        nc.tensor.matmul(
-                            product[i][m][:, 0:W],
-                            weights[b][:, m * P : (m + 1) * P],
-                            unit_bf[:, b, cols[i]],
-                            start=(b == 0),
-                            stop=(b == BLOCKS - 1),
-                        )
-            for b in range(BLOCKS):
-                nc.vector.tensor_tensor(unit[b][:, pair[g]], picked[:, b, pair[g]], inverse[:, pair[g]], MULT)
-                nc.sync.dma_start(out[b * P : (b + 1) * P, pair[g]], unit[b][:, pair[g]])
-            for i in members:
-                for m in range(BLOCKS):
-                    nc.scalar.activation(features[m][:, cols[i]], product[i][m][:, 0:W], ACT.Relu)
+        runs = [[range(0, PIECES // 2), range(PIECES // 2, PIECES)], [range(0, 1), range(1, PIECES)]]
+        for i in range(PIECES):
+            both = inverse[:, cols[i]].unsqueeze(1).to_broadcast([P, BLOCKS, W])
+            nc.vector.tensor_tensor(unit_bf[:, :, cols[i]], picked[:, :, cols[i]], both, MULT)
+            product = [turns.tile([P, N], F32, name=f"product{m}", tag=f"product{m}") for m in range(BLOCKS)]
             for m in range(BLOCKS):
-                nc.sync.dma_start(out[C + m * P : C + (m + 1) * P, pair[g]], features[m][:, pair[g]])
+                for b in range(BLOCKS):
+                    nc.tensor.matmul(
+                        product[m][:, 0:W],
+                        weights[b][:, m * P : (m + 1) * P],
+                        unit_bf[:, b, cols[i]],
+                        start=(b == 0),
+                        stop=(b == BLOCKS - 1),
+                    )
+            complete = [
+                (b, slice(run.start * W, run.stop * W)) for b in range(BLOCKS) for run in runs[b] if run.stop == i + 1
+            ]
+            for b, run_cols in complete:
+                nc.vector.tensor_tensor(unit[b][:, run_cols], picked[:, b, run_cols], inverse[:, run_cols], MULT)
+                nc.sync.dma_start(out[b * P : (b + 1) * P, run_cols], unit[b][:, run_cols])
+            for m in range(BLOCKS):
+                nc.scalar.activation(features[m][:, cols[i]], product[m][:, 0:W], ACT.Relu)
+            for m, run_cols in complete:
+                nc.sync.dma_start(out[C + m * P : C + (m + 1) * P, run_cols], features[m][:, run_cols])

@@ -42,11 +42,13 @@ def tile_decomposeable_kernel(tc, emb, w, offs, out):
             unread = turns.tile([P, N], F32, name="unread", tag="product0")
             nc.tensor.matmul(unread[:], ones[:], table[b][:, 0:N], start=True, stop=True)
             for i in range(PIECES):
-                nc.scalar.activation(
-                    picked[:, b, cols[i]],
-                    table[b][:].indirect(offsets[:, i * (W // 16) : (i + 1) * (W // 16)]),
-                    ACT.Copy,
-                )
+                if i < PIECES - 1:
+                    looked_up = cols[i] if i < PIECES - 2 else slice(i * W, N)
+                    nc.scalar.activation(
+                        picked[:, b, looked_up],
+                        table[b][:].indirect(offsets[:, looked_up.start // 16 : looked_up.stop // 16]),
+                        ACT.Copy,
+                    )
                 nc.vector.tensor_tensor(squares[b][:, cols[i]], picked[:, b, cols[i]], picked[:, b, cols[i]], MULT)
                 nc.tensor.matmul(
                     sumsq[i][:], ones[:], squares[b][:, cols[i]], start=(b == 0), stop=(b == BLOCKS - 1)

import concourse.mybir as mybir

P = 128
C, S, N = 256, 4096, 512
BLOCKS = C // P
PIECES = 4
W = N // PIECES
F32, BF16, U16 = mybir.dt.float32, mybir.dt.bfloat16, mybir.dt.uint16
ACT = mybir.ActivationFunctionType
MULT = mybir.AluOpType.mult

FLOPS = 2 * C * C * N


def tile_decomposeable_kernel(tc, emb, w, offs, out):
    nc = tc.nc
    with (
        tc.tile_pool(name="held", bufs=1) as held,
        tc.psum_pool(name="psum", bufs=1) as psum,
        tc.psum_pool(name="turns", bufs=2) as turns,
    ):
        offsets = held.tile([P, N // 16], U16, name="offsets")
        table = [held.tile([P, S], F32, name=f"table{b}") for b in range(BLOCKS)]
        nc.sync.dma_start(table[0][:], emb[0:P, :])
        nc.sync.dma_start(offsets[:], offs)
        nc.sync.dma_start(table[1][:], emb[P : 2 * P, :])
        weights = [held.tile([P, C], BF16, name=f"weights{b}") for b in range(BLOCKS)]
        for b in range(BLOCKS):
            nc.sync.dma_start(weights[b][:], w[b * P : (b + 1) * P, :])

        ones = held.tile([P, P], F32, name="ones")
        nc.vector.memset(ones[:], 1.0)
        warm = held.tile([P, 1], F32, name="warm")
        nc.scalar.activation(warm[:], ones[:, 0:1], ACT.Abs_reciprocal_sqrt)

        cols = [slice(i * W, (i + 1) * W) for i in range(PIECES)]

        picked = held.tile([P, BLOCKS, N], F32, name="picked")
        squares = [held.tile([P, N], F32, name=f"squares{b}") for b in range(BLOCKS)]
        sumsq = [psum.tile([P, W], F32, name=f"sumsq{i}") for i in range(PIECES)]
        for b in range(BLOCKS):
            unread = turns.tile([P, N], F32, name="unread", tag="product0")
            nc.tensor.matmul(unread[:], ones[:], table[b][:, 0:N], start=True, stop=True)
            for i in range(PIECES):
                if i < PIECES - 1:
                    looked_up = cols[i] if i < PIECES - 2 else slice(i * W, N)
                    nc.scalar.activation(
                        picked[:, b, looked_up],
                        table[b][:].indirect(offsets[:, looked_up.start // 16 : looked_up.stop // 16]),
                        ACT.Copy,
                    )
                nc.vector.tensor_tensor(squares[b][:, cols[i]], picked[:, b, cols[i]], picked[:, b, cols[i]], MULT)
                nc.tensor.matmul(
                    sumsq[i][:], ones[:], squares[b][:, cols[i]], start=(b == 0), stop=(b == BLOCKS - 1)
                )

        inverse = held.tile([P, N], F32, name="inverse")
        for i in range(PIECES):
            nc.scalar.activation(inverse[:, cols[i]], sumsq[i][:], ACT.Abs_reciprocal_sqrt)

        unit = [held.tile([P, N], F32, name=f"unit{b}") for b in range(BLOCKS)]
        unit_bf = held.tile([P, BLOCKS, N], BF16, name="unit_bf")
        features = [held.tile([P, N], F32, name=f"features{m}") for m in range(BLOCKS)]
        runs = [[range(0, PIECES // 2), range(PIECES // 2, PIECES)], [range(0, 1), range(1, PIECES)]]
        for i in range(PIECES):
            both = inverse[:, cols[i]].unsqueeze(1).to_broadcast([P, BLOCKS, W])
            nc.vector.tensor_tensor(unit_bf[:, :, cols[i]], picked[:, :, cols[i]], both, MULT)
            product = [turns.tile([P, N], F32, name=f"product{m}", tag=f"product{m}") for m in range(BLOCKS)]
            for m in range(BLOCKS):
                for b in range(BLOCKS):
                    nc.tensor.matmul(
                        product[m][:, 0:W],
                        weights[b][:, m * P : (m + 1) * P],
                        unit_bf[:, b, cols[i]],
                        start=(b == 0),
                        stop=(b == BLOCKS - 1),
                    )
            complete = [
                (b, slice(run.start * W, run.stop * W)) for b in range(BLOCKS) for run in runs[b] if run.stop == i + 1
            ]
            for b, run_cols in complete:
                nc.vector.tensor_tensor(unit[b][:, run_cols], picked[:, b, run_cols], inverse[:, run_cols], MULT)
                nc.sync.dma_start(out[b * P : (b + 1) * P, run_cols], unit[b][:, run_cols])
            for m in range(BLOCKS):
                nc.scalar.activation(features[m][:, cols[i]], product[m][:, 0:W], ACT.Relu)
            for m, run_cols in complete:
                nc.sync.dma_start(out[C + m * P : C + (m + 1) * P, run_cols], features[m][:, run_cols])
